import numpy as np
import ml_dtypes


def mxq(x, axis, fmt="e4m3"):
    dtype, down = {"e4m3": (ml_dtypes.float8_e4m3fn, 7), "e5m2": (ml_dtypes.float8_e5m2, 14)}[fmt]
    v = np.moveaxis(np.asarray(x, np.float32).astype(ml_dtypes.bfloat16).astype(np.float64), axis, -1)
    blocks = v.reshape(v.shape[:-1] + (-1, 32))
    amax = np.abs(blocks).max(-1, keepdims=True)
    byte = np.maximum(np.where(amax > 0, np.frexp(amax)[1] - 1 + 127, 0) - down, 1)
    scale = np.exp2(byte - 127.0)
    codes = (blocks / scale).astype(np.float32).astype(dtype).astype(np.float64)
    return np.moveaxis((codes * scale).reshape(v.shape), -1, axis)


WIDE = False


def mx_kscale(k):
    if not WIDE:
        return np.ones(k)
    levels = np.array([10, -10, 5, -5, 0])
    a = np.random.permutation(np.resize(levels, k // 512 * 4)).reshape(k // 512, 4)
    idx = np.arange(k)
    return np.exp2(a[idx // 512, idx % 128 // 32])


BF16 = ml_dtypes.bfloat16


def bf(x):
    return np.asarray(x, np.float32).astype(BF16)


def f64(x):
    return np.asarray(x).astype(np.float64)


E2M1 = np.array([0.0, 0.5, 1.0, 1.5, 2.0, 3.0, 4.0, 6.0, -0.0, -0.5, -1.0, -1.5, -2.0, -3.0, -4.0, -6.0])


def pack_weight(w, fmt):
    k, n = w.shape
    w = f64(bf(w)).reshape(k // 32, 32, n)
    amax = np.abs(w).max(1)
    if fmt == "e4m3":
        byte = np.frexp(amax)[1] - 1 + 127 - 7
    else:
        mant, ex = np.frexp(amax / 6.0)
        byte = np.where(mant > 0.5, ex, ex - 1) + 127
    byte = np.clip(np.where(amax > 0, byte, 1), 1, 254)
    scaled = (w * np.exp2(127.0 - byte)[:, None, :]).reshape(k, n).astype(np.float32)
    by_word = np.ascontiguousarray(scaled.reshape(k // 512, 128, 4, n).transpose(0, 1, 3, 2))
    if fmt == "e4m3":
        words = by_word.astype(ml_dtypes.float8_e4m3fn).view(np.uint8)
    else:
        c = by_word.astype(ml_dtypes.float4_e2m1fn).view(np.uint8) & 0xF
        words = c[..., 0::2] | (c[..., 1::2] << 4)
    return np.ascontiguousarray(words), np.ascontiguousarray(byte.astype(np.uint8).reshape(k // 512, 16, n))


def unpack_weight(words, scales, fmt):
    g, p, n, _ = words.shape
    if fmt == "e4m3":
        vals = np.ascontiguousarray(words).view(ml_dtypes.float8_e4m3fn).astype(np.float64)
    else:
        nib = np.empty((g, p, n, 4), np.uint8)
        nib[..., 0::2] = words & 0xF
        nib[..., 1::2] = words >> 4
        vals = E2M1[nib]
    vals = vals * np.repeat(np.exp2(scales.astype(np.float64) - 127.0), 8, axis=1)[..., None]
    return vals.transpose(0, 1, 3, 2).reshape(g * 512, n)

def pack4(w):
    words, scales = pack_weight(w, "e2m1")
    return words.reshape(words.shape[0], 128, -1), scales


def unpack4(words, scales):
    return unpack_weight(words.reshape(words.shape[0], 128, -1, 2), scales, "e2m1")


B, N, D, L = 1, 1024, 512, 512
SEGS = N // L


def setup_inputs():
    s = mx_kscale(D)
    col = np.concatenate([np.full(D, np.sqrt(SEGS)), np.ones(D)])
    x = bf(np.random.standard_normal((B, N, D)) * s)
    words, scales = pack4(np.random.standard_normal((D, D + D)) * col / np.sqrt(D) / s[:, None])
    return {"x": x, "w_kv_words": words, "w_kv_scales": scales}


def reference(x, w_kv_words, w_kv_scales):
    kv = mxq(f64(x), 2, "e4m3") @ unpack4(w_kv_words, w_kv_scales)
    k, v = kv[..., :D], kv[..., D:]
    keys_lm = k.reshape(B, L, SEGS, D).mean(axis=2)
    vals_lm = v.reshape(B, L, SEGS, D).mean(axis=2)
    return v, keys_lm, vals_lm

@@ -1,0 +1,135 @@
+from contextlib import ExitStack
+
+import concourse.mybir as mybir
+from concourse.masks import make_identity
+
+F32 = mybir.dt.float32
+BF16 = mybir.dt.bfloat16
+I32 = mybir.dt.int32
+U32 = mybir.dt.uint32
+U8 = mybir.dt.uint8
+FP8X4 = mybir.dt.float8_e4m3fn_x4
+FP4X4 = mybir.dt.float4_e2m1fn_x4
+
+P = 128
+TOKENS = 1024
+K = 512
+D = 512
+PAIR = 2
+CHUNK = P * PAIR
+CHUNKS = TOKENS // CHUNK
+WORDS = K // 2
+HALVES = 2
+KEYS = 0
+VALUES = 1
+
+FLOPS = 2 * TOKENS * K * (D + D)
+
+
+def tile_ammattention_pa_kernel(tc, x, w_kv_words, w_kv_scales, out_0, out_1, out_2):
+    nc = tc.nc
+
+    x_chunks = x[0].rearrange("(c p e) k -> c p (e k)", p=P, e=PAIR)
+    v_chunks = out_0[0].rearrange("(c p e) d -> c p (e d)", p=P, e=PAIR)
+    keys_lm_chunks = out_1[0].rearrange("(c p) d -> c p d", p=P)
+    vals_lm_chunks = out_2[0].rearrange("(c p) d -> c p d", p=P)
+
+    with ExitStack() as ctx:
+        ctx.enter_context(tc.manual_schedule())
+        keep = ctx.enter_context(tc.tile_pool(name="keep", bufs=1))
+        banks = ctx.enter_context(tc.psum_pool(name="banks", bufs=8))
+
+        identity = keep.tile([P, P], F32)
+        table_warmer = keep.tile([P, 1], F32)
+        x_rows = keep.tile([P, CHUNKS, PAIR * K], BF16)
+        x_grouped = keep.tile([P, CHUNKS, CHUNK * 4], BF16, align_bytes=64)
+        x_codes = keep.tile([P, CHUNKS, CHUNK], U32, align_bytes=64)
+        x_scales = keep.tile([P, CHUNKS, CHUNK], U8, align_bytes=64)
+        w_words = keep.tile([P, 2 * (D + D)], U8, align_bytes=64)
+        w_scales = keep.tile([P, D + D], U8, align_bytes=64)
+        v_rows = keep.tile([P, CHUNKS, PAIR, D], F32)
+        keys_lm_rows = keep.tile([P, CHUNKS, D], F32)
+        vals_lm_rows = keep.tile([P, CHUNKS, D], F32)
+
+        nc.vector.memset(w_scales[:].bitcast(I32), 0)
+        nc.vector.memset(table_warmer[:], 0.0)
+        nc.scalar.mul(out=table_warmer[:], in_=table_warmer[:], mul=0.5)
+        make_identity(nc, identity[:])
+
+        def load_x(c):
+            nc.sync.dma_start(out=x_rows[:, c, :], in_=x_chunks[c])
+
+        def load_w_words(half):
+            cols = slice(2 * D * half, 2 * D * (half + 1))
+            nc.sync.dma_start(out=w_words[:, cols].bitcast(I32), in_=w_kv_words[0, :, cols].bitcast(I32))
+
+        load_x(0)
+        for r in range(4):
+            nc.sync.dma_start(
+                out=w_scales[r:P:32, :].bitcast(I32), in_=w_kv_scales[0, r:16:4, :].bitcast(I32)
+            )
+        load_w_words(VALUES)
+        for c in range(1, CHUNKS):
+            load_x(c)
+        load_w_words(KEYS)
+
+        def quantise_chunk(c):
+            words = x_rows[:, c, :].bitcast(F32)
+            flipped = banks.tile([P, PAIR * HALVES * P], F32, tag="bank")
+            for e in range(PAIR):
+                for h in range(HALVES):
+                    nc.tensor.transpose(
+                        flipped[:, (HALVES * e + h) * P : (HALVES * e + h + 1) * P],
+                        words[:, WORDS * e + h : WORDS * (e + 1) : HALVES],
+                        identity[:],
+                    )
+            nc.scalar.copy(
+                out=x_grouped[:, c, :].bitcast(F32).rearrange("p (e m h) -> p e m h", e=PAIR, h=HALVES),
+                in_=flipped[:].rearrange("p (e h m) -> p e m h", e=PAIR, h=HALVES),
+            )
+            nc.vector.quantize_mx(
+                out=x_codes[:, c, :].bitcast(FP8X4), scales=x_scales[:, c, :], in_=x_grouped[:, c, :]
+            )
+
+        def mx_pass(acc, c, e, half, start, stop):
+            tokens = slice(P * e, P * (e + 1))
+            nc.tensor.matmul_mx(
+                out=acc[:],
+                lhsT=x_codes[:, c, tokens].bitcast(FP8X4),
+                lhsT_scale=x_scales[:, c, tokens],
+                rhs=w_words[:, 2 * D * half : 2 * D * (half + 1)].bitcast(FP4X4),
+                rhs_scale=w_scales[:, D * half : D * (half + 1)],
+                start=start,
+                stop=stop,
+            )
+
+        def values_of_chunk(c):
+            v_even = banks.tile([P, D], F32, tag="bank")
+            mx_pass(v_even, c, 0, VALUES, True, True)
+            v_odd = banks.tile([P, D], F32, tag="bank")
+            mx_pass(v_odd, c, 1, VALUES, True, True)
+            nc.scalar.copy(out=v_rows[:, c, 0, :], in_=v_even[:])
+            nc.vector.tensor_copy(out=v_rows[:, c, 1, :], in_=v_odd[:])
+            nc.sync.dma_start(out=v_chunks[c], in_=v_rows[:, c, :, :].rearrange("p e d -> p (e d)"))
+
+        def pair_sum(c, half):
+            acc = banks.tile([P, D], F32, tag="bank")
+            mx_pass(acc, c, 0, half, True, False)
+            mx_pass(acc, c, 1, half, False, True)
+            return acc
+
+        def means_of_chunk(c):
+            key_sum = pair_sum(c, KEYS)
+            val_sum = pair_sum(c, VALUES)
+            nc.vector.tensor_scalar_mul(out=keys_lm_rows[:, c, :], in0=key_sum[:], scalar1=1.0 / PAIR)
+            nc.sync.dma_start(out=keys_lm_chunks[c], in_=keys_lm_rows[:, c, :])
+            nc.scalar.mul(out=vals_lm_rows[:, c, :], in_=val_sum[:], mul=1.0 / PAIR)
+            nc.sync.dma_start(out=vals_lm_chunks[c], in_=vals_lm_rows[:, c, :])
+
+        quantise_chunk(0)
+        for c in range(1, CHUNKS):
+            quantise_chunk(c)
+            values_of_chunk(c - 1)
+        values_of_chunk(CHUNKS - 1)
+        for c in range(CHUNKS):
+            means_of_chunk(c)

@@ -22,6 +22,7 @@ WORDS = K // 2
 HALVES = 2
 KEYS = 0
 VALUES = 1
+WARM_UP_MATMULS = 6
 
 FLOPS = 2 * TOKENS * K * (D + D)
 
@@ -41,6 +42,7 @@ def tile_ammattention_pa_kernel(tc, x, w_kv_words, w_kv_scales, out_0, out_1, ou
 
         identity = keep.tile([P, P], F32)
         table_warmer = keep.tile([P, 1], F32)
+        zeros = keep.tile([P, D], BF16)
         x_rows = keep.tile([P, CHUNKS, PAIR * K], BF16)
         x_grouped = keep.tile([P, CHUNKS, CHUNK * 4], BF16, align_bytes=64)
         x_codes = keep.tile([P, CHUNKS, CHUNK], U32, align_bytes=64)
@@ -52,9 +54,13 @@ def tile_ammattention_pa_kernel(tc, x, w_kv_words, w_kv_scales, out_0, out_1, ou
         vals_lm_rows = keep.tile([P, CHUNKS, D], F32)
 
         nc.vector.memset(w_scales[:].bitcast(I32), 0)
+        nc.vector.memset(zeros[:], 0.0)
         nc.vector.memset(table_warmer[:], 0.0)
         nc.scalar.mul(out=table_warmer[:], in_=table_warmer[:], mul=0.5)
         make_identity(nc, identity[:])
+        warm_up = banks.tile([P, D], F32, tag="bank")
+        for i in range(WARM_UP_MATMULS):
+            nc.tensor.matmul(out=warm_up[:], lhsT=zeros[:, 0:P], rhs=zeros[:], start=True, stop=True)
 
         def load_x(c):
             nc.sync.dma_start(out=x_rows[:, c, :], in_=x_chunks[c])

@@ -16,13 +16,14 @@ TOKENS = 1024
 K = 512
 D = 512
 PAIR = 2
-CHUNK = P * PAIR
-CHUNKS = TOKENS // CHUNK
+EVEN = 0
+ODD = 1
+CHUNKS = TOKENS // (P * PAIR)
+PACK = 4
 WORDS = K // 2
 HALVES = 2
 KEYS = 0
 VALUES = 1
-WARM_UP_MATMULS = 6
 
 FLOPS = 2 * TOKENS * K * (D + D)
 
@@ -30,10 +31,10 @@ FLOPS = 2 * TOKENS * K * (D + D)
 def tile_ammattention_pa_kernel(tc, x, w_kv_words, w_kv_scales, out_0, out_1, out_2):
     nc = tc.nc
 
-    x_chunks = x[0].rearrange("(c p e) k -> c p (e k)", p=P, e=PAIR)
-    v_chunks = out_0[0].rearrange("(c p e) d -> c p (e d)", p=P, e=PAIR)
-    keys_lm_chunks = out_1[0].rearrange("(c p) d -> c p d", p=P)
-    vals_lm_chunks = out_2[0].rearrange("(c p) d -> c p d", p=P)
+    x_dram = x[0].rearrange("(p c e) k -> p c (e k)", c=CHUNKS, e=PAIR)
+    v_dram = out_0[0].rearrange("(p c e) d -> p c e d", c=CHUNKS, e=PAIR)
+    keys_lm_dram = out_1[0].rearrange("(p c) d -> p c d", c=CHUNKS)
+    vals_lm_dram = out_2[0].rearrange("(p c) d -> p c d", c=CHUNKS)
 
     with ExitStack() as ctx:
         ctx.enter_context(tc.manual_schedule())
@@ -42,11 +43,10 @@ def tile_ammattention_pa_kernel(tc, x, w_kv_words, w_kv_scales, out_0, out_1, ou
 
         identity = keep.tile([P, P], F32)
         table_warmer = keep.tile([P, 1], F32)
-        zeros = keep.tile([P, D], BF16)
-        x_rows = keep.tile([P, CHUNKS, PAIR * K], BF16)
-        x_grouped = keep.tile([P, CHUNKS, CHUNK * 4], BF16, align_bytes=64)
-        x_codes = keep.tile([P, CHUNKS, CHUNK], U32, align_bytes=64)
-        x_scales = keep.tile([P, CHUNKS, CHUNK], U8, align_bytes=64)
+        x_rows = keep.tile([P, CHUNKS, PAIR, K], BF16)
+        x_grouped = keep.tile([P, CHUNKS, PAIR, P * PACK], BF16, align_bytes=64)
+        x_codes = keep.tile([P, CHUNKS, PAIR, P], U32, align_bytes=64)
+        x_scales = keep.tile([P, CHUNKS, PAIR, P], U8, align_bytes=64)
         w_words = keep.tile([P, 2 * (D + D)], U8, align_bytes=64)
         w_scales = keep.tile([P, D + D], U8, align_bytes=64)
         v_rows = keep.tile([P, CHUNKS, PAIR, D], F32)
@@ -54,88 +54,86 @@ def tile_ammattention_pa_kernel(tc, x, w_kv_words, w_kv_scales, out_0, out_1, ou
         vals_lm_rows = keep.tile([P, CHUNKS, D], F32)
 
         nc.vector.memset(w_scales[:].bitcast(I32), 0)
-        nc.vector.memset(zeros[:], 0.0)
         nc.vector.memset(table_warmer[:], 0.0)
         nc.scalar.mul(out=table_warmer[:], in_=table_warmer[:], mul=0.5)
         make_identity(nc, identity[:])
-        warm_up = banks.tile([P, D], F32, tag="bank")
-        for i in range(WARM_UP_MATMULS):
-            nc.tensor.matmul(out=warm_up[:], lhsT=zeros[:, 0:P], rhs=zeros[:], start=True, stop=True)
 
-        def load_x(c):
-            nc.sync.dma_start(out=x_rows[:, c, :], in_=x_chunks[c])
+        def load_x(first, count):
+            chunks = slice(first, first + count)
+            nc.sync.dma_start(out=x_rows[:, chunks, :, :].rearrange("p c e k -> p c (e k)"), in_=x_dram[:, chunks, :])
 
-        def load_w_words(half):
-            cols = slice(2 * D * half, 2 * D * (half + 1))
-            nc.sync.dma_start(out=w_words[:, cols].bitcast(I32), in_=w_kv_words[0, :, cols].bitcast(I32))
-
-        load_x(0)
+        load_x(0, 1)
+        load_x(1, 1)
+        nc.sync.dma_start(out=w_words[:].bitcast(I32), in_=w_kv_words[0].bitcast(I32))
         for r in range(4):
             nc.sync.dma_start(
                 out=w_scales[r:P:32, :].bitcast(I32), in_=w_kv_scales[0, r:16:4, :].bitcast(I32)
             )
-        load_w_words(VALUES)
-        for c in range(1, CHUNKS):
-            load_x(c)
-        load_w_words(KEYS)
+        load_x(2, CHUNKS - 2)
 
-        def quantise_chunk(c):
-            words = x_rows[:, c, :].bitcast(F32)
-            flipped = banks.tile([P, PAIR * HALVES * P], F32, tag="bank")
-            for e in range(PAIR):
-                for h in range(HALVES):
-                    nc.tensor.transpose(
-                        flipped[:, (HALVES * e + h) * P : (HALVES * e + h + 1) * P],
-                        words[:, WORDS * e + h : WORDS * (e + 1) : HALVES],
-                        identity[:],
-                    )
+        def transpose_tokens(c, e):
+            words = x_rows[:, c, e, :].bitcast(F32)
+            flipped = banks.tile([P, HALVES * P], F32, tag="bank")
+            for h in range(HALVES):
+                nc.tensor.transpose(flipped[:, h * P : (h + 1) * P], words[:, h:WORDS:HALVES], identity[:])
+            return flipped
+
+        def regroup_tokens(c, e, flipped):
             nc.scalar.copy(
-                out=x_grouped[:, c, :].bitcast(F32).rearrange("p (e m h) -> p e m h", e=PAIR, h=HALVES),
-                in_=flipped[:].rearrange("p (e h m) -> p e m h", e=PAIR, h=HALVES),
+                out=x_grouped[:, c, e, :].bitcast(F32).rearrange("p (m h) -> p m h", h=HALVES),
+                in_=flipped[:].rearrange("p (h m) -> p m h", h=HALVES),
             )
+
+        def quantise_tokens(c, e):
             nc.vector.quantize_mx(
-                out=x_codes[:, c, :].bitcast(FP8X4), scales=x_scales[:, c, :], in_=x_grouped[:, c, :]
+                out=x_codes[:, c, e, :].bitcast(FP8X4), scales=x_scales[:, c, e, :], in_=x_grouped[:, c, e, :]
             )
 
         def mx_pass(acc, c, e, half, start, stop):
-            tokens = slice(P * e, P * (e + 1))
             nc.tensor.matmul_mx(
                 out=acc[:],
-                lhsT=x_codes[:, c, tokens].bitcast(FP8X4),
-                lhsT_scale=x_scales[:, c, tokens],
+                lhsT=x_codes[:, c, e, :].bitcast(FP8X4),
+                lhsT_scale=x_scales[:, c, e, :],
                 rhs=w_words[:, 2 * D * half : 2 * D * (half + 1)].bitcast(FP4X4),
                 rhs_scale=w_scales[:, D * half : D * (half + 1)],
                 start=start,
                 stop=stop,
             )
 
-        def values_of_chunk(c):
-            v_even = banks.tile([P, D], F32, tag="bank")
-            mx_pass(v_even, c, 0, VALUES, True, True)
-            v_odd = banks.tile([P, D], F32, tag="bank")
-            mx_pass(v_odd, c, 1, VALUES, True, True)
-            nc.scalar.copy(out=v_rows[:, c, 0, :], in_=v_even[:])
-            nc.vector.tensor_copy(out=v_rows[:, c, 1, :], in_=v_odd[:])
-            nc.sync.dma_start(out=v_chunks[c], in_=v_rows[:, c, :, :].rearrange("p e d -> p (e d)"))
+        flipped_even = transpose_tokens(0, EVEN)
+        flipped_odd = transpose_tokens(0, ODD)
+        regroup_tokens(0, EVEN, flipped_even)
+        quantise_tokens(0, EVEN)
+        regroup_tokens(0, ODD, flipped_odd)
+        quantise_tokens(0, ODD)
 
-        def pair_sum(c, half):
-            acc = banks.tile([P, D], F32, tag="bank")
-            mx_pass(acc, c, 0, half, True, False)
-            mx_pass(acc, c, 1, half, False, True)
-            return acc
-
-        def means_of_chunk(c):
-            key_sum = pair_sum(c, KEYS)
-            val_sum = pair_sum(c, VALUES)
-            nc.vector.tensor_scalar_mul(out=keys_lm_rows[:, c, :], in0=key_sum[:], scalar1=1.0 / PAIR)
-            nc.sync.dma_start(out=keys_lm_chunks[c], in_=keys_lm_rows[:, c, :])
-            nc.scalar.mul(out=vals_lm_rows[:, c, :], in_=val_sum[:], mul=1.0 / PAIR)
-            nc.sync.dma_start(out=vals_lm_chunks[c], in_=vals_lm_rows[:, c, :])
-
-        quantise_chunk(0)
-        for c in range(1, CHUNKS):
-            quantise_chunk(c)
-            values_of_chunk(c - 1)
-        values_of_chunk(CHUNKS - 1)
         for c in range(CHUNKS):
-            means_of_chunk(c)
+            more = c + 1 < CHUNKS
+            if more:
+                flipped_even = transpose_tokens(c + 1, EVEN)
+                flipped_odd = transpose_tokens(c + 1, ODD)
+            v_even = banks.tile([P, D], F32, tag="bank")
+            mx_pass(v_even, c, EVEN, VALUES, True, True)
+            v_odd = banks.tile([P, D], F32, tag="bank")
+            mx_pass(v_odd, c, ODD, VALUES, True, True)
+            key_sum = banks.tile([P, D], F32, tag="bank")
+            mx_pass(key_sum, c, EVEN, KEYS, True, False)
+            mx_pass(key_sum, c, ODD, KEYS, False, True)
+
+            if more:
+                regroup_tokens(c + 1, EVEN, flipped_even)
+                quantise_tokens(c + 1, EVEN)
+                regroup_tokens(c + 1, ODD, flipped_odd)
+                quantise_tokens(c + 1, ODD)
+
+            nc.scalar.copy(out=v_rows[:, c, EVEN, :], in_=v_even[:])
+            nc.sync.dma_start(out=v_dram[:, c, EVEN, :], in_=v_rows[:, c, EVEN, :])
+            nc.vector.tensor_copy(out=v_rows[:, c, ODD, :], in_=v_odd[:])
+            nc.sync.dma_start(out=v_dram[:, c, ODD, :], in_=v_rows[:, c, ODD, :])
+
+            nc.scalar.mul(out=keys_lm_rows[:, c, :], in_=key_sum[:], mul=1.0 / PAIR)
+            nc.sync.dma_start(out=keys_lm_dram[:, c, :], in_=keys_lm_rows[:, c, :])
+
+            nc.vector.tensor_add(out=vals_lm_rows[:, c, :], in0=v_rows[:, c, EVEN, :], in1=v_rows[:, c, ODD, :])
+            nc.vector.tensor_scalar_mul(out=vals_lm_rows[:, c, :], in0=vals_lm_rows[:, c, :], scalar1=1.0 / PAIR)
+            nc.sync.dma_start(out=vals_lm_dram[:, c, :], in_=vals_lm_rows[:, c, :])

@@ -16,9 +16,9 @@ TOKENS = 1024
 K = 512
 D = 512
 PAIR = 2
-EVEN = 0
-ODD = 1
-CHUNKS = TOKENS // (P * PAIR)
+CHUNKS = 2
+SETS = TOKENS // (P * CHUNKS)
+SEGS = SETS // PAIR
 PACK = 4
 WORDS = K // 2
 HALVES = 2
@@ -31,10 +31,10 @@ FLOPS = 2 * TOKENS * K * (D + D)
 def tile_ammattention_pa_kernel(tc, x, w_kv_words, w_kv_scales, out_0, out_1, out_2):
     nc = tc.nc
 
-    x_dram = x[0].rearrange("(p c e) k -> p c (e k)", c=CHUNKS, e=PAIR)
-    v_dram = out_0[0].rearrange("(p c e) d -> p c e d", c=CHUNKS, e=PAIR)
-    keys_lm_dram = out_1[0].rearrange("(p c) d -> p c d", c=CHUNKS)
-    vals_lm_dram = out_2[0].rearrange("(p c) d -> p c d", c=CHUNKS)
+    x_dram = x[0].rearrange("(p t) k -> p t k", t=CHUNKS * SETS)
+    v_dram = out_0[0].rearrange("(p c s) d -> p c s d", c=CHUNKS, s=SETS)
+    keys_lm_dram = out_1[0].rearrange("(p c g) d -> p c g d", c=CHUNKS, g=SEGS)
+    vals_lm_dram = out_2[0].rearrange("(p c g) d -> p c g d", c=CHUNKS, g=SEGS)
 
     with ExitStack() as ctx:
         ctx.enter_context(tc.manual_schedule())
@@ -43,15 +43,15 @@ def tile_ammattention_pa_kernel(tc, x, w_kv_words, w_kv_scales, out_0, out_1, ou
 
         identity = keep.tile([P, P], F32)
         table_warmer = keep.tile([P, 1], F32)
-        x_rows = keep.tile([P, CHUNKS, PAIR, K], BF16)
-        x_grouped = keep.tile([P, CHUNKS, PAIR, P * PACK], BF16, align_bytes=64)
-        x_codes = keep.tile([P, CHUNKS, PAIR, P], U32, align_bytes=64)
-        x_scales = keep.tile([P, CHUNKS, PAIR, P], U8, align_bytes=64)
+        x_rows = keep.tile([P, CHUNKS, SETS, K], BF16)
+        x_grouped = keep.tile([P, CHUNKS, SETS, P * PACK], BF16, align_bytes=64)
+        x_codes = keep.tile([P, CHUNKS, SETS, P], U32, align_bytes=64)
+        x_scales = keep.tile([P, CHUNKS, SETS, P], U8, align_bytes=64)
         w_words = keep.tile([P, 2 * (D + D)], U8, align_bytes=64)
         w_scales = keep.tile([P, D + D], U8, align_bytes=64)
-        v_rows = keep.tile([P, CHUNKS, PAIR, D], F32)
-        keys_lm_rows = keep.tile([P, CHUNKS, D], F32)
-        vals_lm_rows = keep.tile([P, CHUNKS, D], F32)
+        v_rows = keep.tile([P, CHUNKS, SETS, D], F32)
+        keys_lm_rows = keep.tile([P, CHUNKS, SEGS, D], F32)
+        vals_lm_rows = keep.tile([P, CHUNKS, SEGS, D], F32)
 
         nc.vector.memset(w_scales[:].bitcast(I32), 0)
         nc.vector.memset(table_warmer[:], 0.0)
@@ -59,81 +59,89 @@ def tile_ammattention_pa_kernel(tc, x, w_kv_words, w_kv_scales, out_0, out_1, ou
         make_identity(nc, identity[:])
 
         def load_x(first, count):
-            chunks = slice(first, first + count)
-            nc.sync.dma_start(out=x_rows[:, chunks, :, :].rearrange("p c e k -> p c (e k)"), in_=x_dram[:, chunks, :])
+            rows = slice(first, first + count)
+            nc.sync.dma_start(out=x_rows[:].rearrange("p c s k -> p (c s) k")[:, rows, :], in_=x_dram[:, rows, :])
 
         load_x(0, 1)
         load_x(1, 1)
+        load_x(2, 2)
         nc.sync.dma_start(out=w_words[:].bitcast(I32), in_=w_kv_words[0].bitcast(I32))
         for r in range(4):
             nc.sync.dma_start(
                 out=w_scales[r:P:32, :].bitcast(I32), in_=w_kv_scales[0, r:16:4, :].bitcast(I32)
             )
-        load_x(2, CHUNKS - 2)
+        load_x(4, 4)
 
-        def transpose_tokens(c, e):
-            words = x_rows[:, c, e, :].bitcast(F32)
+        def transpose_set(c, s):
+            words = x_rows[:, c, s, :].bitcast(F32)
             flipped = banks.tile([P, HALVES * P], F32, tag="bank")
             for h in range(HALVES):
                 nc.tensor.transpose(flipped[:, h * P : (h + 1) * P], words[:, h:WORDS:HALVES], identity[:])
             return flipped
 
-        def regroup_tokens(c, e, flipped):
+        def quantise_set(c, s, flipped):
             nc.scalar.copy(
-                out=x_grouped[:, c, e, :].bitcast(F32).rearrange("p (m h) -> p m h", h=HALVES),
+                out=x_grouped[:, c, s, :].bitcast(F32).rearrange("p (m h) -> p m h", h=HALVES),
                 in_=flipped[:].rearrange("p (h m) -> p m h", h=HALVES),
             )
-
-        def quantise_tokens(c, e):
             nc.vector.quantize_mx(
-                out=x_codes[:, c, e, :].bitcast(FP8X4), scales=x_scales[:, c, e, :], in_=x_grouped[:, c, e, :]
+                out=x_codes[:, c, s, :].bitcast(FP8X4), scales=x_scales[:, c, s, :], in_=x_grouped[:, c, s, :]
             )
 
-        def mx_pass(acc, c, e, half, start, stop):
+        def mx_pass(acc, c, s, columns, start, stop):
             nc.tensor.matmul_mx(
                 out=acc[:],
-                lhsT=x_codes[:, c, e, :].bitcast(FP8X4),
-                lhsT_scale=x_scales[:, c, e, :],
-                rhs=w_words[:, 2 * D * half : 2 * D * (half + 1)].bitcast(FP4X4),
-                rhs_scale=w_scales[:, D * half : D * (half + 1)],
+                lhsT=x_codes[:, c, s, :].bitcast(FP8X4),
+                lhsT_scale=x_scales[:, c, s, :],
+                rhs=w_words[:, 2 * D * columns : 2 * D * (columns + 1)].bitcast(FP4X4),
+                rhs_scale=w_scales[:, D * columns : D * (columns + 1)],
                 start=start,
                 stop=stop,
             )
 
-        flipped_even = transpose_tokens(0, EVEN)
-        flipped_odd = transpose_tokens(0, ODD)
-        regroup_tokens(0, EVEN, flipped_even)
-        quantise_tokens(0, EVEN)
-        regroup_tokens(0, ODD, flipped_odd)
-        quantise_tokens(0, ODD)
+        flipped_sets = [transpose_set(0, s) for s in range(SETS)]
+        for s in range(SETS):
+            quantise_set(0, s, flipped_sets[s])
 
         for c in range(CHUNKS):
             more = c + 1 < CHUNKS
+
+            for g in range(SEGS):
+                even = PAIR * g
+                odd = PAIR * g + 1
+                v_even = banks.tile([P, D], F32, tag="bank")
+                mx_pass(v_even, c, even, VALUES, True, True)
+                v_odd = banks.tile([P, D], F32, tag="bank")
+                mx_pass(v_odd, c, odd, VALUES, True, True)
+                nc.scalar.copy(out=v_rows[:, c, even, :], in_=v_even[:])
+                nc.vector.tensor_copy(out=v_rows[:, c, odd, :], in_=v_odd[:])
+                if c == 0 and g == 0:
+                    nc.sync.dma_start(out=v_dram[:, c, even, :], in_=v_rows[:, c, even, :])
+                    nc.sync.dma_start(out=v_dram[:, c, odd, :], in_=v_rows[:, c, odd, :])
+                else:
+                    nc.sync.dma_start(out=v_dram[:, c, even : odd + 1, :], in_=v_rows[:, c, even : odd + 1, :])
+
+            key_sums = []
+            for g in range(SEGS):
+                key_sum = banks.tile([P, D], F32, tag="bank")
+                mx_pass(key_sum, c, PAIR * g, KEYS, True, False)
+                mx_pass(key_sum, c, PAIR * g + 1, KEYS, False, True)
+                key_sums.append(key_sum)
             if more:
-                flipped_even = transpose_tokens(c + 1, EVEN)
-                flipped_odd = transpose_tokens(c + 1, ODD)
-            v_even = banks.tile([P, D], F32, tag="bank")
-            mx_pass(v_even, c, EVEN, VALUES, True, True)
-            v_odd = banks.tile([P, D], F32, tag="bank")
-            mx_pass(v_odd, c, ODD, VALUES, True, True)
-            key_sum = banks.tile([P, D], F32, tag="bank")
-            mx_pass(key_sum, c, EVEN, KEYS, True, False)
-            mx_pass(key_sum, c, ODD, KEYS, False, True)
+                flipped_sets = [transpose_set(c + 1, s) for s in range(SETS)]
+
+            for g in range(SEGS):
+                nc.scalar.mul(out=keys_lm_rows[:, c, g, :], in_=key_sums[g][:], mul=1.0 / PAIR)
+            nc.sync.dma_start(out=keys_lm_dram[:, c, :, :], in_=keys_lm_rows[:, c, :, :])
+
+            nc.vector.tensor_add(
+                out=vals_lm_rows[:, c, :, :], in0=v_rows[:, c, 0:SETS:PAIR, :], in1=v_rows[:, c, 1:SETS:PAIR, :]
+            )
+            nc.vector.tensor_scalar_mul(
+                out=vals_lm_rows[:, c, :, :], in0=vals_lm_rows[:, c, :, :], scalar1=1.0 / PAIR
+            )
+            nc.sync.dma_start(out=vals_lm_dram[:, c, :, :], in_=vals_lm_rows[:, c, :, :])
 
             if more:
-                regroup_tokens(c + 1, EVEN, flipped_even)
-                quantise_tokens(c + 1, EVEN)
-                regroup_tokens(c + 1, ODD, flipped_odd)
-                quantise_tokens(c + 1, ODD)
-
-            nc.scalar.copy(out=v_rows[:, c, EVEN, :], in_=v_even[:])
-            nc.sync.dma_start(out=v_dram[:, c, EVEN, :], in_=v_rows[:, c, EVEN, :])
-            nc.vector.tensor_copy(out=v_rows[:, c, ODD, :], in_=v_odd[:])
-            nc.sync.dma_start(out=v_dram[:, c, ODD, :], in_=v_rows[:, c, ODD, :])
-
-            nc.scalar.mul(out=keys_lm_rows[:, c, :], in_=key_sum[:], mul=1.0 / PAIR)
-            nc.sync.dma_start(out=keys_lm_dram[:, c, :], in_=keys_lm_rows[:, c, :])
-
-            nc.vector.tensor_add(out=vals_lm_rows[:, c, :], in0=v_rows[:, c, EVEN, :], in1=v_rows[:, c, ODD, :])
-            nc.vector.tensor_scalar_mul(out=vals_lm_rows[:, c, :], in0=vals_lm_rows[:, c, :], scalar1=1.0 / PAIR)
-            nc.sync.dma_start(out=vals_lm_dram[:, c, :], in_=vals_lm_rows[:, c, :])
+                for s in range(SETS):
+                    quantise_set(c + 1, s, flipped_sets[s])

@@ -16,9 +16,9 @@ TOKENS = 1024
 K = 512
 D = 512
 PAIR = 2
-CHUNKS = 2
-SETS = TOKENS // (P * CHUNKS)
-SEGS = SETS // PAIR
+EVEN = 0
+ODD = 1
+CHUNKS = TOKENS // (P * PAIR)
 PACK = 4
 WORDS = K // 2
 HALVES = 2
@@ -31,10 +31,10 @@ FLOPS = 2 * TOKENS * K * (D + D)
 def tile_ammattention_pa_kernel(tc, x, w_kv_words, w_kv_scales, out_0, out_1, out_2):
     nc = tc.nc
 
-    x_dram = x[0].rearrange("(p t) k -> p t k", t=CHUNKS * SETS)
-    v_dram = out_0[0].rearrange("(p c s) d -> p c s d", c=CHUNKS, s=SETS)
-    keys_lm_dram = out_1[0].rearrange("(p c g) d -> p c g d", c=CHUNKS, g=SEGS)
-    vals_lm_dram = out_2[0].rearrange("(p c g) d -> p c g d", c=CHUNKS, g=SEGS)
+    x_dram = x[0].rearrange("(p t) k -> p t k", t=CHUNKS * PAIR)
+    v_dram = out_0[0].rearrange("(p c e) d -> p c e d", c=CHUNKS, e=PAIR)
+    keys_lm_dram = out_1[0].rearrange("(p c) d -> p c d", c=CHUNKS)
+    vals_lm_dram = out_2[0].rearrange("(p c) d -> p c d", c=CHUNKS)
 
     with ExitStack() as ctx:
         ctx.enter_context(tc.manual_schedule())
@@ -43,15 +43,15 @@ def tile_ammattention_pa_kernel(tc, x, w_kv_words, w_kv_scales, out_0, out_1, ou
 
         identity = keep.tile([P, P], F32)
         table_warmer = keep.tile([P, 1], F32)
-        x_rows = keep.tile([P, CHUNKS, SETS, K], BF16)
-        x_grouped = keep.tile([P, CHUNKS, SETS, P * PACK], BF16, align_bytes=64)
-        x_codes = keep.tile([P, CHUNKS, SETS, P], U32, align_bytes=64)
-        x_scales = keep.tile([P, CHUNKS, SETS, P], U8, align_bytes=64)
+        x_rows = keep.tile([P, CHUNKS, PAIR, K], BF16)
+        x_grouped = keep.tile([P, CHUNKS, PAIR, P * PACK], BF16, align_bytes=64)
+        x_codes = keep.tile([P, CHUNKS, PAIR, P], U32, align_bytes=64)
+        x_scales = keep.tile([P, CHUNKS, PAIR, P], U8, align_bytes=64)
         w_words = keep.tile([P, 2 * (D + D)], U8, align_bytes=64)
         w_scales = keep.tile([P, D + D], U8, align_bytes=64)
-        v_rows = keep.tile([P, CHUNKS, SETS, D], F32)
-        keys_lm_rows = keep.tile([P, CHUNKS, SEGS, D], F32)
-        vals_lm_rows = keep.tile([P, CHUNKS, SEGS, D], F32)
+        v_rows = keep.tile([P, CHUNKS, PAIR, D], F32)
+        keys_lm_rows = keep.tile([P, CHUNKS, D], F32)
+        vals_lm_rows = keep.tile([P, CHUNKS, D], F32)
 
         nc.vector.memset(w_scales[:].bitcast(I32), 0)
         nc.vector.memset(table_warmer[:], 0.0)
@@ -60,7 +60,7 @@ def tile_ammattention_pa_kernel(tc, x, w_kv_words, w_kv_scales, out_0, out_1, ou
 
         def load_x(first, count):
             rows = slice(first, first + count)
-            nc.sync.dma_start(out=x_rows[:].rearrange("p c s k -> p (c s) k")[:, rows, :], in_=x_dram[:, rows, :])
+            nc.sync.dma_start(out=x_rows[:].rearrange("p c e k -> p (c e) k")[:, rows, :], in_=x_dram[:, rows, :])
 
         load_x(0, 1)
         load_x(1, 1)
@@ -72,76 +72,75 @@ def tile_ammattention_pa_kernel(tc, x, w_kv_words, w_kv_scales, out_0, out_1, ou
             )
         load_x(4, 4)
 
-        def transpose_set(c, s):
-            words = x_rows[:, c, s, :].bitcast(F32)
-            flipped = banks.tile([P, HALVES * P], F32, tag="bank")
-            for h in range(HALVES):
-                nc.tensor.transpose(flipped[:, h * P : (h + 1) * P], words[:, h:WORDS:HALVES], identity[:])
+        def transpose_sets(c, first, count):
+            flipped = banks.tile([P, count * HALVES * P], F32, tag="bank")
+            for i in range(count):
+                words = x_rows[:, c, first + i, :].bitcast(F32)
+                for h in range(HALVES):
+                    column = (i * HALVES + h) * P
+                    nc.tensor.transpose(flipped[:, column : column + P], words[:, h:WORDS:HALVES], identity[:])
             return flipped
 
-        def quantise_set(c, s, flipped):
+        def regroup_sets(c, first, count, flipped):
+            grouped = x_grouped[:, c, first : first + count, :].rearrange("p e n -> p (e n)").bitcast(F32)
             nc.scalar.copy(
-                out=x_grouped[:, c, s, :].bitcast(F32).rearrange("p (m h) -> p m h", h=HALVES),
-                in_=flipped[:].rearrange("p (h m) -> p m h", h=HALVES),
-            )
-            nc.vector.quantize_mx(
-                out=x_codes[:, c, s, :].bitcast(FP8X4), scales=x_scales[:, c, s, :], in_=x_grouped[:, c, s, :]
+                out=grouped.rearrange("p (e m h) -> p e m h", e=count, h=HALVES),
+                in_=flipped[:].rearrange("p (e h m) -> p e m h", e=count, h=HALVES),
             )
 
-        def mx_pass(acc, c, s, columns, start, stop):
+        def quantise_sets(c, first, count):
+            sets = slice(first, first + count)
+            nc.vector.quantize_mx(
+                out=x_codes[:, c, sets, :].rearrange("p e m -> p (e m)").bitcast(FP8X4),
+                scales=x_scales[:, c, sets, :].rearrange("p e m -> p (e m)"),
+                in_=x_grouped[:, c, sets, :].rearrange("p e n -> p (e n)"),
+            )
+
+        def mx_pass(acc, c, e, half, start, stop):
             nc.tensor.matmul_mx(
                 out=acc[:],
-                lhsT=x_codes[:, c, s, :].bitcast(FP8X4),
-                lhsT_scale=x_scales[:, c, s, :],
-                rhs=w_words[:, 2 * D * columns : 2 * D * (columns + 1)].bitcast(FP4X4),
-                rhs_scale=w_scales[:, D * columns : D * (columns + 1)],
+                lhsT=x_codes[:, c, e, :].bitcast(FP8X4),
+                lhsT_scale=x_scales[:, c, e, :],
+                rhs=w_words[:, 2 * D * half : 2 * D * (half + 1)].bitcast(FP4X4),
+                rhs_scale=w_scales[:, D * half : D * (half + 1)],
                 start=start,
                 stop=stop,
             )
 
-        flipped_sets = [transpose_set(0, s) for s in range(SETS)]
-        for s in range(SETS):
-            quantise_set(0, s, flipped_sets[s])
+        flipped_even = transpose_sets(0, EVEN, 1)
+        flipped_odd = transpose_sets(0, ODD, 1)
+        regroup_sets(0, EVEN, 1, flipped_even)
+        quantise_sets(0, EVEN, 1)
+        regroup_sets(0, ODD, 1, flipped_odd)
+        quantise_sets(0, ODD, 1)
 
         for c in range(CHUNKS):
             more = c + 1 < CHUNKS
-
-            for g in range(SEGS):
-                even = PAIR * g
-                odd = PAIR * g + 1
-                v_even = banks.tile([P, D], F32, tag="bank")
-                mx_pass(v_even, c, even, VALUES, True, True)
-                v_odd = banks.tile([P, D], F32, tag="bank")
-                mx_pass(v_odd, c, odd, VALUES, True, True)
-                nc.scalar.copy(out=v_rows[:, c, even, :], in_=v_even[:])
-                nc.vector.tensor_copy(out=v_rows[:, c, odd, :], in_=v_odd[:])
-                if c == 0 and g == 0:
-                    nc.sync.dma_start(out=v_dram[:, c, even, :], in_=v_rows[:, c, even, :])
-                    nc.sync.dma_start(out=v_dram[:, c, odd, :], in_=v_rows[:, c, odd, :])
-                else:
-                    nc.sync.dma_start(out=v_dram[:, c, even : odd + 1, :], in_=v_rows[:, c, even : odd + 1, :])
-
-            key_sums = []
-            for g in range(SEGS):
-                key_sum = banks.tile([P, D], F32, tag="bank")
-                mx_pass(key_sum, c, PAIR * g, KEYS, True, False)
-                mx_pass(key_sum, c, PAIR * g + 1, KEYS, False, True)
-                key_sums.append(key_sum)
             if more:
-                flipped_sets = [transpose_set(c + 1, s) for s in range(SETS)]
-
-            for g in range(SEGS):
-                nc.scalar.mul(out=keys_lm_rows[:, c, g, :], in_=key_sums[g][:], mul=1.0 / PAIR)
-            nc.sync.dma_start(out=keys_lm_dram[:, c, :, :], in_=keys_lm_rows[:, c, :, :])
-
-            nc.vector.tensor_add(
-                out=vals_lm_rows[:, c, :, :], in0=v_rows[:, c, 0:SETS:PAIR, :], in1=v_rows[:, c, 1:SETS:PAIR, :]
-            )
-            nc.vector.tensor_scalar_mul(
-                out=vals_lm_rows[:, c, :, :], in0=vals_lm_rows[:, c, :, :], scalar1=1.0 / PAIR
-            )
-            nc.sync.dma_start(out=vals_lm_dram[:, c, :, :], in_=vals_lm_rows[:, c, :, :])
+                flipped = transpose_sets(c + 1, EVEN, PAIR)
+            v_even = banks.tile([P, D], F32, tag="bank")
+            mx_pass(v_even, c, EVEN, VALUES, True, True)
+            v_odd = banks.tile([P, D], F32, tag="bank")
+            mx_pass(v_odd, c, ODD, VALUES, True, True)
+            key_sum = banks.tile([P, D], F32, tag="bank")
+            mx_pass(key_sum, c, EVEN, KEYS, True, False)
+            mx_pass(key_sum, c, ODD, KEYS, False, True)
 
             if more:
-                for s in range(SETS):
-                    quantise_set(c + 1, s, flipped_sets[s])
+                regroup_sets(c + 1, EVEN, PAIR, flipped)
+            nc.scalar.copy(out=v_rows[:, c, EVEN, :], in_=v_even[:])
+            nc.vector.tensor_copy(out=v_rows[:, c, ODD, :], in_=v_odd[:])
+            if c == 0:
+                nc.sync.dma_start(out=v_dram[:, c, EVEN, :], in_=v_rows[:, c, EVEN, :])
+                nc.sync.dma_start(out=v_dram[:, c, ODD, :], in_=v_rows[:, c, ODD, :])
+            else:
+                nc.sync.dma_start(out=v_dram[:, c, :, :], in_=v_rows[:, c, :, :])
+            if more:
+                quantise_sets(c + 1, EVEN, PAIR)
+
+            nc.scalar.mul(out=keys_lm_rows[:, c, :], in_=key_sum[:], mul=1.0 / PAIR)
+            nc.sync.dma_start(out=keys_lm_dram[:, c, :], in_=keys_lm_rows[:, c, :])
+
+            nc.vector.tensor_add(out=vals_lm_rows[:, c, :], in0=v_rows[:, c, EVEN, :], in1=v_rows[:, c, ODD, :])
+            nc.vector.tensor_scalar_mul(out=vals_lm_rows[:, c, :], in0=vals_lm_rows[:, c, :], scalar1=1.0 / PAIR)
+            nc.sync.dma_start(out=vals_lm_dram[:, c, :], in_=vals_lm_rows[:, c, :])

@@ -24,6 +24,7 @@ WORDS = K // 2
 HALVES = 2
 KEYS = 0
 VALUES = 1
+WARM_MATMULS = 6
 
 FLOPS = 2 * TOKENS * K * (D + D)
 
@@ -52,11 +53,16 @@ def tile_ammattention_pa_kernel(tc, x, w_kv_words, w_kv_scales, out_0, out_1, ou
         v_rows = keep.tile([P, CHUNKS, PAIR, D], F32)
         keys_lm_rows = keep.tile([P, CHUNKS, D], F32)
         vals_lm_rows = keep.tile([P, CHUNKS, D], F32)
+        zeros = keep.tile([P, D], BF16)
 
+        nc.vector.memset(zeros[:], 0.0)
         nc.vector.memset(w_scales[:].bitcast(I32), 0)
         nc.vector.memset(table_warmer[:], 0.0)
         nc.scalar.mul(out=table_warmer[:], in_=table_warmer[:], mul=0.5)
         make_identity(nc, identity[:])
+        warm_bank = banks.tile([P, D], F32, tag="bank")
+        for i in range(WARM_MATMULS):
+            nc.tensor.matmul(out=warm_bank[:], lhsT=zeros[:, 0:P], rhs=zeros[:], start=True, stop=True)
 
         def load_x(first, count):
             rows = slice(first, first + count)

@@ -24,7 +24,7 @@ WORDS = K // 2
 HALVES = 2
 KEYS = 0
 VALUES = 1
-WARM_MATMULS = 6
+WARM_MATMULS = 4
 
 FLOPS = 2 * TOKENS * K * (D + D)
 
@@ -53,16 +53,16 @@ def tile_ammattention_pa_kernel(tc, x, w_kv_words, w_kv_scales, out_0, out_1, ou
         v_rows = keep.tile([P, CHUNKS, PAIR, D], F32)
         keys_lm_rows = keep.tile([P, CHUNKS, D], F32)
         vals_lm_rows = keep.tile([P, CHUNKS, D], F32)
-        zeros = keep.tile([P, D], BF16)
+        zeros = keep.tile([P, P], F32)
 
-        nc.vector.memset(zeros[:], 0.0)
+        nc.gpsimd.memset(zeros[:], 0.0)
         nc.vector.memset(w_scales[:].bitcast(I32), 0)
         nc.vector.memset(table_warmer[:], 0.0)
         nc.scalar.mul(out=table_warmer[:], in_=table_warmer[:], mul=0.5)
         make_identity(nc, identity[:])
-        warm_bank = banks.tile([P, D], F32, tag="bank")
+        warm_bank = banks.tile([P, P], F32, tag="bank")
         for i in range(WARM_MATMULS):
-            nc.tensor.matmul(out=warm_bank[:], lhsT=zeros[:, 0:P], rhs=zeros[:], start=True, stop=True)
+            nc.tensor.matmul(out=warm_bank[:], lhsT=zeros[:], rhs=zeros[:], start=True, stop=True)
 
         def load_x(first, count):
             rows = slice(first, first + count)

@@ -25,6 +25,7 @@ HALVES = 2
 KEYS = 0
 VALUES = 1
 WARM_MATMULS = 4
+FIRST_PARTS = 2
 
 FLOPS = 2 * TOKENS * K * (D + D)
 
@@ -102,13 +103,14 @@ def tile_ammattention_pa_kernel(tc, x, w_kv_words, w_kv_scales, out_0, out_1, ou
                 in_=x_grouped[:, c, sets, :].rearrange("p e n -> p (e n)"),
             )
 
-        def mx_pass(acc, c, e, half, start, stop):
+        def mx_pass(acc, c, e, half, start, stop, first=0, count=D):
+            low = D * half + first
             nc.tensor.matmul_mx(
                 out=acc[:],
                 lhsT=x_codes[:, c, e, :].bitcast(FP8X4),
                 lhsT_scale=x_scales[:, c, e, :],
-                rhs=w_words[:, 2 * D * half : 2 * D * (half + 1)].bitcast(FP4X4),
-                rhs_scale=w_scales[:, D * half : D * (half + 1)],
+                rhs=w_words[:, 2 * low : 2 * (low + count)].bitcast(FP4X4),
+                rhs_scale=w_scales[:, low : low + count],
                 start=start,
                 stop=stop,
             )
@@ -124,22 +126,34 @@ def tile_ammattention_pa_kernel(tc, x, w_kv_words, w_kv_scales, out_0, out_1, ou
             more = c + 1 < CHUNKS
             if more:
                 flipped = transpose_sets(c + 1, EVEN, PAIR)
-            v_even = banks.tile([P, D], F32, tag="bank")
-            mx_pass(v_even, c, EVEN, VALUES, True, True)
+            if c == 0:
+                v_even_parts = []
+                for i in range(FIRST_PARTS):
+                    part = banks.tile([P, D // FIRST_PARTS], F32, tag="bank")
+                    mx_pass(part, c, EVEN, VALUES, True, True, first=i * (D // FIRST_PARTS), count=D // FIRST_PARTS)
+                    v_even_parts.append(part)
+            else:
+                v_even = banks.tile([P, D], F32, tag="bank")
+                mx_pass(v_even, c, EVEN, VALUES, True, True)
             v_odd = banks.tile([P, D], F32, tag="bank")
             mx_pass(v_odd, c, ODD, VALUES, True, True)
             key_sum = banks.tile([P, D], F32, tag="bank")
             mx_pass(key_sum, c, EVEN, KEYS, True, False)
             mx_pass(key_sum, c, ODD, KEYS, False, True)
 
-            if more:
-                regroup_sets(c + 1, EVEN, PAIR, flipped)
-            nc.scalar.copy(out=v_rows[:, c, EVEN, :], in_=v_even[:])
-            nc.vector.tensor_copy(out=v_rows[:, c, ODD, :], in_=v_odd[:])
             if c == 0:
-                nc.sync.dma_start(out=v_dram[:, c, EVEN, :], in_=v_rows[:, c, EVEN, :])
+                for i in range(FIRST_PARTS):
+                    columns = slice(i * (D // FIRST_PARTS), (i + 1) * (D // FIRST_PARTS))
+                    nc.vector.tensor_copy(out=v_rows[:, c, EVEN, columns], in_=v_even_parts[i][:])
+                    nc.sync.dma_start(out=v_dram[:, c, EVEN, columns], in_=v_rows[:, c, EVEN, columns])
+                regroup_sets(c + 1, EVEN, PAIR, flipped)
+                nc.scalar.copy(out=v_rows[:, c, ODD, :], in_=v_odd[:])
                 nc.sync.dma_start(out=v_dram[:, c, ODD, :], in_=v_rows[:, c, ODD, :])
             else:
+                if more:
+                    regroup_sets(c + 1, EVEN, PAIR, flipped)
+                nc.scalar.copy(out=v_rows[:, c, EVEN, :], in_=v_even[:])
+                nc.vector.tensor_copy(out=v_rows[:, c, ODD, :], in_=v_odd[:])
                 nc.sync.dma_start(out=v_dram[:, c, :, :], in_=v_rows[:, c, :, :])
             if more:
                 quantise_sets(c + 1, EVEN, PAIR)

@@ -77,7 +77,8 @@ def tile_ammattention_pa_kernel(tc, x, w_kv_words, w_kv_scales, out_0, out_1, ou
             nc.sync.dma_start(
                 out=w_scales[r:P:32, :].bitcast(I32), in_=w_kv_scales[0, r:16:4, :].bitcast(I32)
             )
-        load_x(4, 4)
+        load_x(4, 2)
+        load_x(6, 2)
 
         def transpose_sets(c, first, count):
             flipped = banks.tile([P, count * HALVES * P], F32, tag="bank")

from contextlib import ExitStack

import concourse.mybir as mybir
from concourse.masks import make_identity

F32 = mybir.dt.float32
BF16 = mybir.dt.bfloat16
I32 = mybir.dt.int32
U32 = mybir.dt.uint32
U8 = mybir.dt.uint8
FP8X4 = mybir.dt.float8_e4m3fn_x4
FP4X4 = mybir.dt.float4_e2m1fn_x4

P = 128
TOKENS = 1024
K = 512
D = 512
PAIR = 2
EVEN = 0
ODD = 1
CHUNKS = TOKENS // (P * PAIR)
PACK = 4
WORDS = K // 2
HALVES = 2
KEYS = 0
VALUES = 1
WARM_MATMULS = 4
FIRST_PARTS = 2

FLOPS = 2 * TOKENS * K * (D + D)


def tile_ammattention_pa_kernel(tc, x, w_kv_words, w_kv_scales, out_0, out_1, out_2):
    nc = tc.nc

    x_dram = x[0].rearrange("(p t) k -> p t k", t=CHUNKS * PAIR)
    v_dram = out_0[0].rearrange("(p c e) d -> p c e d", c=CHUNKS, e=PAIR)
    keys_lm_dram = out_1[0].rearrange("(p c) d -> p c d", c=CHUNKS)
    vals_lm_dram = out_2[0].rearrange("(p c) d -> p c d", c=CHUNKS)

    with ExitStack() as ctx:
        ctx.enter_context(tc.manual_schedule())
        keep = ctx.enter_context(tc.tile_pool(name="keep", bufs=1))
        banks = ctx.enter_context(tc.psum_pool(name="banks", bufs=8))

        identity = keep.tile([P, P], F32)
        table_warmer = keep.tile([P, 1], F32)
        x_rows = keep.tile([P, CHUNKS, PAIR, K], BF16)
        x_grouped = keep.tile([P, CHUNKS, PAIR, P * PACK], BF16, align_bytes=64)
        x_codes = keep.tile([P, CHUNKS, PAIR, P], U32, align_bytes=64)
        x_scales = keep.tile([P, CHUNKS, PAIR, P], U8, align_bytes=64)
        w_words = keep.tile([P, 2 * (D + D)], U8, align_bytes=64)
        w_scales = keep.tile([P, D + D], U8, align_bytes=64)
        v_rows = keep.tile([P, CHUNKS, PAIR, D], F32)
        keys_lm_rows = keep.tile([P, CHUNKS, D], F32)
        vals_lm_rows = keep.tile([P, CHUNKS, D], F32)
        zeros = keep.tile([P, P], F32)

        nc.gpsimd.memset(zeros[:], 0.0)
        nc.vector.memset(w_scales[:].bitcast(I32), 0)
        nc.vector.memset(table_warmer[:], 0.0)
        nc.scalar.mul(out=table_warmer[:], in_=table_warmer[:], mul=0.5)
        make_identity(nc, identity[:])
        warm_bank = banks.tile([P, P], F32, tag="bank")
        for i in range(WARM_MATMULS):
            nc.tensor.matmul(out=warm_bank[:], lhsT=zeros[:], rhs=zeros[:], start=True, stop=True)

        def load_x(first, count):
            rows = slice(first, first + count)
            nc.sync.dma_start(out=x_rows[:].rearrange("p c e k -> p (c e) k")[:, rows, :], in_=x_dram[:, rows, :])

        load_x(0, 1)
        load_x(1, 1)
        load_x(2, 2)
        nc.sync.dma_start(out=w_words[:].bitcast(I32), in_=w_kv_words[0].bitcast(I32))
        for r in range(4):
            nc.sync.dma_start(
                out=w_scales[r:P:32, :].bitcast(I32), in_=w_kv_scales[0, r:16:4, :].bitcast(I32)
            )
        load_x(4, 2)
        load_x(6, 2)

        def transpose_sets(c, first, count):
            flipped = banks.tile([P, count * HALVES * P], F32, tag="bank")
            for i in range(count):
                words = x_rows[:, c, first + i, :].bitcast(F32)
                for h in range(HALVES):
                    column = (i * HALVES + h) * P
                    nc.tensor.transpose(flipped[:, column : column + P], words[:, h:WORDS:HALVES], identity[:])
            return flipped

        def regroup_sets(c, first, count, flipped):
            grouped = x_grouped[:, c, first : first + count, :].rearrange("p e n -> p (e n)").bitcast(F32)
            nc.scalar.copy(
                out=grouped.rearrange("p (e m h) -> p e m h", e=count, h=HALVES),
                in_=flipped[:].rearrange("p (e h m) -> p e m h", e=count, h=HALVES),
            )

        def quantise_sets(c, first, count):
            sets = slice(first, first + count)
            nc.vector.quantize_mx(
                out=x_codes[:, c, sets, :].rearrange("p e m -> p (e m)").bitcast(FP8X4),
                scales=x_scales[:, c, sets, :].rearrange("p e m -> p (e m)"),
                in_=x_grouped[:, c, sets, :].rearrange("p e n -> p (e n)"),
            )

        def mx_pass(acc, c, e, half, start, stop, first=0, count=D):
            low = D * half + first
            nc.tensor.matmul_mx(
                out=acc[:],
                lhsT=x_codes[:, c, e, :].bitcast(FP8X4),
                lhsT_scale=x_scales[:, c, e, :],
                rhs=w_words[:, 2 * low : 2 * (low + count)].bitcast(FP4X4),
                rhs_scale=w_scales[:, low : low + count],
                start=start,
                stop=stop,
            )

        flipped_even = transpose_sets(0, EVEN, 1)
        flipped_odd = transpose_sets(0, ODD, 1)
        regroup_sets(0, EVEN, 1, flipped_even)
        quantise_sets(0, EVEN, 1)
        regroup_sets(0, ODD, 1, flipped_odd)
        quantise_sets(0, ODD, 1)

        for c in range(CHUNKS):
            more = c + 1 < CHUNKS
            if more:
                flipped = transpose_sets(c + 1, EVEN, PAIR)
            if c == 0:
                v_even_parts = []
                for i in range(FIRST_PARTS):
                    part = banks.tile([P, D // FIRST_PARTS], F32, tag="bank")
                    mx_pass(part, c, EVEN, VALUES, True, True, first=i * (D // FIRST_PARTS), count=D // FIRST_PARTS)
                    v_even_parts.append(part)
            else:
                v_even = banks.tile([P, D], F32, tag="bank")
                mx_pass(v_even, c, EVEN, VALUES, True, True)
            v_odd = banks.tile([P, D], F32, tag="bank")
            mx_pass(v_odd, c, ODD, VALUES, True, True)
            key_sum = banks.tile([P, D], F32, tag="bank")
            mx_pass(key_sum, c, EVEN, KEYS, True, False)
            mx_pass(key_sum, c, ODD, KEYS, False, True)

            if c == 0:
                for i in range(FIRST_PARTS):
                    columns = slice(i * (D // FIRST_PARTS), (i + 1) * (D // FIRST_PARTS))
                    nc.vector.tensor_copy(out=v_rows[:, c, EVEN, columns], in_=v_even_parts[i][:])
                    nc.sync.dma_start(out=v_dram[:, c, EVEN, columns], in_=v_rows[:, c, EVEN, columns])
                regroup_sets(c + 1, EVEN, PAIR, flipped)
                nc.scalar.copy(out=v_rows[:, c, ODD, :], in_=v_odd[:])
                nc.sync.dma_start(out=v_dram[:, c, ODD, :], in_=v_rows[:, c, ODD, :])
            else:
                if more:
                    regroup_sets(c + 1, EVEN, PAIR, flipped)
                nc.scalar.copy(out=v_rows[:, c, EVEN, :], in_=v_even[:])
                nc.vector.tensor_copy(out=v_rows[:, c, ODD, :], in_=v_odd[:])
                nc.sync.dma_start(out=v_dram[:, c, :, :], in_=v_rows[:, c, :, :])
            if more:
                quantise_sets(c + 1, EVEN, PAIR)

            nc.scalar.mul(out=keys_lm_rows[:, c, :], in_=key_sum[:], mul=1.0 / PAIR)
            nc.sync.dma_start(out=keys_lm_dram[:, c, :], in_=keys_lm_rows[:, c, :])

            nc.vector.tensor_add(out=vals_lm_rows[:, c, :], in0=v_rows[:, c, EVEN, :], in1=v_rows[:, c, ODD, :])
            nc.vector.tensor_scalar_mul(out=vals_lm_rows[:, c, :], in0=vals_lm_rows[:, c, :], scalar1=1.0 / PAIR)
            nc.sync.dma_start(out=vals_lm_dram[:, c, :], in_=vals_lm_rows[:, c, :])
